import numpy as np
import ml_dtypes


def mxq(x, axis, fmt="e4m3"):
    dtype, down = {"e4m3": (ml_dtypes.float8_e4m3fn, 7), "e5m2": (ml_dtypes.float8_e5m2, 14)}[fmt]
    v = np.moveaxis(np.asarray(x, np.float32).astype(ml_dtypes.bfloat16).astype(np.float64), axis, -1)
    blocks = v.reshape(v.shape[:-1] + (-1, 32))
    amax = np.abs(blocks).max(-1, keepdims=True)
    byte = np.maximum(np.where(amax > 0, np.frexp(amax)[1] - 1 + 127, 0) - down, 1)
    scale = np.exp2(byte - 127.0)
    codes = (blocks / scale).astype(np.float32).astype(dtype).astype(np.float64)
    return np.moveaxis((codes * scale).reshape(v.shape), -1, axis)


WIDE = False


def mx_kscale(k):
    if not WIDE:
        return np.ones(k)
    levels = np.array([10, -10, 5, -5, 0])
    a = np.random.permutation(np.resize(levels, k // 512 * 4)).reshape(k // 512, 4)
    idx = np.arange(k)
    return np.exp2(a[idx // 512, idx % 128 // 32])


BF16 = ml_dtypes.bfloat16


def bf(x):
    return np.asarray(x, np.float32).astype(BF16)


def f64(x):
    return np.asarray(x).astype(np.float64)


E2M1 = np.array([0.0, 0.5, 1.0, 1.5, 2.0, 3.0, 4.0, 6.0, -0.0, -0.5, -1.0, -1.5, -2.0, -3.0, -4.0, -6.0])


def pack_weight(w, fmt):
    k, n = w.shape
    w = f64(bf(w)).reshape(k // 32, 32, n)
    amax = np.abs(w).max(1)
    if fmt == "e4m3":
        byte = np.frexp(amax)[1] - 1 + 127 - 7
    else:
        mant, ex = np.frexp(amax / 6.0)
        byte = np.where(mant > 0.5, ex, ex - 1) + 127
    byte = np.clip(np.where(amax > 0, byte, 1), 1, 254)
    scaled = (w * np.exp2(127.0 - byte)[:, None, :]).reshape(k, n).astype(np.float32)
    by_word = np.ascontiguousarray(scaled.reshape(k // 512, 128, 4, n).transpose(0, 1, 3, 2))
    if fmt == "e4m3":
        words = by_word.astype(ml_dtypes.float8_e4m3fn).view(np.uint8)
    else:
        c = by_word.astype(ml_dtypes.float4_e2m1fn).view(np.uint8) & 0xF
        words = c[..., 0::2] | (c[..., 1::2] << 4)
    return np.ascontiguousarray(words), np.ascontiguousarray(byte.astype(np.uint8).reshape(k // 512, 16, n))


def unpack_weight(words, scales, fmt):
    g, p, n, _ = words.shape
    if fmt == "e4m3":
        vals = np.ascontiguousarray(words).view(ml_dtypes.float8_e4m3fn).astype(np.float64)
    else:
        nib = np.empty((g, p, n, 4), np.uint8)
        nib[..., 0::2] = words & 0xF
        nib[..., 1::2] = words >> 4
        vals = E2M1[nib]
    vals = vals * np.repeat(np.exp2(scales.astype(np.float64) - 127.0), 8, axis=1)[..., None]
    return vals.transpose(0, 1, 3, 2).reshape(g * 512, n)


B, D_IN, UNITS = 1024, 512, 512
FMT = "e4m3"


def sigmoid(v):
    return 1.0 / (1.0 + np.exp(-v))


def setup_inputs():
    s, t = mx_kscale(D_IN), mx_kscale(UNITS)
    sx, sh = 1.0 / np.sqrt(D_IN), 1.0 / np.sqrt(UNITS)
    input_x = bf(np.random.standard_normal((B, D_IN)) * s)
    input_h = bf(np.random.standard_normal((B, UNITS)) * t)
    Wx_r_words, Wx_r_scales = pack_weight(np.random.standard_normal((D_IN, UNITS)) * sx / s[:, None], FMT)
    b_r = bf(np.random.standard_normal(UNITS) * 0.5)
    Wh_r_words, Wh_r_scales = pack_weight(np.random.standard_normal((UNITS, UNITS)) * sh / t[:, None], FMT)
    Wx_h_words, Wx_h_scales = pack_weight(np.random.standard_normal((D_IN, UNITS)) * sx / s[:, None], FMT)
    b_h = bf(np.random.standard_normal(UNITS) * 0.5)
    Wh_h_words, Wh_h_scales = pack_weight(np.random.standard_normal((UNITS, UNITS)) * sh / t[:, None], FMT)
    return {"input_x": input_x,
            "input_h": input_h,
            "Wx_r_words": Wx_r_words,
            "Wx_r_scales": Wx_r_scales,
            "b_r": b_r,
            "Wh_r_words": Wh_r_words,
            "Wh_r_scales": Wh_r_scales,
            "Wx_h_words": Wx_h_words,
            "Wx_h_scales": Wx_h_scales,
            "b_h": b_h,
            "Wh_h_words": Wh_h_words,
            "Wh_h_scales": Wh_h_scales}


def reference(input_x, input_h, Wx_r_words, Wx_r_scales, b_r, Wh_r_words, Wh_r_scales, Wx_h_words, Wx_h_scales, b_h, Wh_h_words, Wh_h_scales):
    xq = mxq(f64(input_x), 1, "e4m3")
    hq = mxq(f64(input_h), 1, "e4m3")
    r = sigmoid((xq @ unpack_weight(Wx_r_words, Wx_r_scales, FMT)) + f64(b_r) + (hq @ unpack_weight(Wh_r_words, Wh_r_scales, FMT)))
    return np.tanh((xq @ unpack_weight(Wx_h_words, Wx_h_scales, FMT)) + f64(b_h) + r * (hq @ unpack_weight(Wh_h_words, Wh_h_scales, FMT)))

@@ -1,0 +1,215 @@
+from contextlib import ExitStack
+
+import concourse.mybir as mybir
+from concourse.masks import make_identity
+
+F32 = mybir.dt.float32
+BF16 = mybir.dt.bfloat16
+I32 = mybir.dt.int32
+U32 = mybir.dt.uint32
+U8 = mybir.dt.uint8
+FP8X4 = mybir.dt.float8_e4m3fn_x4
+ACT = mybir.ActivationFunctionType
+ALU = mybir.AluOpType
+
+P = 128
+PACK = 4
+BATCH = 1024
+FEATURES = P * PACK
+UNITS = 512
+ROWS = BATCH // P
+HALVES = 2
+HALF_ROWS = ROWS // HALVES
+COLS = HALF_ROWS * P
+SLICES = UNITS // P
+PAIRS = HALVES * SLICES // 2
+
+FLOPS = 2 * 4 * BATCH * FEATURES * UNITS
+
+
+def tile_augru_pa_kernel(
+    tc,
+    input_x,
+    input_h,
+    Wx_r_words,
+    Wx_r_scales,
+    b_r,
+    Wh_r_words,
+    Wh_r_scales,
+    Wx_h_words,
+    Wx_h_scales,
+    b_h,
+    Wh_h_words,
+    Wh_h_scales,
+    out,
+):
+    nc = tc.nc
+    weights = {
+        "xr": (Wx_r_words, Wx_r_scales),
+        "hr": (Wh_r_words, Wh_r_scales),
+        "hh": (Wh_h_words, Wh_h_scales),
+        "xh": (Wx_h_words, Wx_h_scales),
+    }
+    activations = {"x": input_x, "h": input_h}
+    out_rows = out.rearrange("(p j) n -> p j n", j=ROWS)
+
+    with ExitStack() as ctx:
+        ctx.enter_context(tc.manual_schedule())
+        keep = ctx.enter_context(tc.tile_pool(name="keep", bufs=1))
+        work = ctx.enter_context(tc.tile_pool(name="work", bufs=4))
+
+        ident = keep.tile([P, P], F32)
+        make_identity(nc, ident[:])
+
+        bias_rows = keep.tile([P, P], BF16)
+        nc.vector.memset(bias_rows[:], 0.0)
+        nc.scalar.dma_start(out=bias_rows[0:SLICES, :], in_=b_r.rearrange("(s u) -> s u", u=P))
+        nc.scalar.dma_start(out=bias_rows[SLICES : 2 * SLICES, :], in_=b_h.rearrange("(s u) -> s u", u=P))
+
+        warm = keep.tile([P, 2], F32)
+        nc.vector.memset(warm[:], 0.0)
+        nc.scalar.activation(out=warm[:, 1:2], in_=warm[:, 0:1], func=ACT.Sigmoid)
+
+        raw = {}
+        w_codes = {}
+        w_scales = {}
+
+        def load_rows(name, half):
+            rows = activations[name].rearrange("(p j) k -> p j k", j=ROWS)
+            raw[name, half] = keep.tile([P, HALF_ROWS, FEATURES], BF16, name="raw_%s%d" % (name, half))
+            nc.sync.dma_start(out=raw[name, half][:], in_=rows[:, half * HALF_ROWS : (half + 1) * HALF_ROWS, :])
+
+        def load_codes(name):
+            w_codes[name] = keep.tile([P, UNITS], U32, name="w_codes_" + name, align_bytes=64)
+            nc.sync.dma_start(
+                out=w_codes[name][:].bitcast(I32),
+                in_=weights[name][0].rearrange("g p n t -> (g p) (n t)").bitcast(I32),
+            )
+
+        def load_scales(name, queue, word):
+            by_r = weights[name][1].rearrange("g (q r) n -> (g r) q n", r=4)
+            for r in range(4):
+                queue.dma_start(out=w_scales[name][r:P:32, :].bitcast(word), in_=by_r[r].bitcast(word))
+
+        for name in weights:
+            w_scales[name] = keep.tile([P, UNITS], U8, name="w_scales_" + name, align_bytes=64)
+            nc.vector.memset(w_scales[name][:].bitcast(I32), 0)
+
+        load_rows("x", 0)
+        load_rows("h", 0)
+        load_scales("xr", nc.sync, I32)
+        load_rows("x", 1)
+        load_rows("h", 1)
+        load_scales("hr", nc.sync, I32)
+        load_scales("hh", nc.gpsimd, F32)
+        for name in weights:
+            load_codes(name)
+        load_scales("xh", nc.sync, I32)
+
+        codes = {}
+        scales = {}
+        grouped = {}
+        bias = keep.tile([P, 2 * SLICES], F32)
+        with tc.psum_pool(name="front_banks", bufs=8) as front_banks:
+            bias_rows_f32 = keep.tile([P, P], F32)
+            nc.vector.tensor_copy(out=bias_rows_f32[:], in_=bias_rows[:])
+            bank = front_banks.tile([P, 2, 2, P], F32)
+            nc.tensor.transpose(bank[:, 0, 0, :], bias_rows_f32[:], ident[:])
+            nc.vector.tensor_copy(out=bias[:], in_=bank[:, 0, 0, 0 : 2 * SLICES])
+
+            waiting = None
+            for half in range(HALVES):
+                for name in ("x", "h"):
+                    grouped[name, half] = keep.tile(
+                        [P, COLS * PACK], BF16, name="grouped_%s%d" % (name, half), align_bytes=64
+                    )
+                    pairs_out = grouped[name, half][:].bitcast(F32).rearrange(
+                        "p (j b u) -> p j b u", j=HALF_ROWS, u=2
+                    )
+                    for first in range(0, HALF_ROWS, 2):
+                        bank = front_banks.tile([P, 2, 2, P], F32)
+                        for j in range(2):
+                            pairs_in = raw[name, half][:, first + j, :].bitcast(F32)
+                            for u in range(2):
+                                nc.tensor.transpose(bank[:, j, u, :], pairs_in[:, u : FEATURES // 2 : 2], ident[:])
+                        copy_out = nc.vector.tensor_copy if first == 0 else nc.scalar.copy
+                        copy_out(
+                            out=pairs_out[:, first : first + 2],
+                            in_=bank[:].rearrange("p j u b -> p j b u"),
+                        )
+                    if waiting is not None:
+                        quantise(nc, keep, waiting, grouped, codes, scales)
+                    waiting = (name, half)
+            quantise(nc, keep, waiting, grouped, codes, scales)
+
+        with tc.psum_pool(name="gate_banks", bufs=2, reuse_waits="tile") as gate_banks:
+            before_tanh = {}
+            for pair in range(PAIRS + 1):
+                if pair < PAIRS:
+                    half = pair // (SLICES // 2)
+                    slices = [2 * (pair % (SLICES // 2)), 2 * (pair % (SLICES // 2)) + 1]
+
+                    reset = {}
+                    state = {}
+                    cand = {}
+                    for s in slices:
+                        reset[s] = gate_banks.tile([P, COLS], F32, name="reset")
+                        state[s] = gate_banks.tile([P, COLS], F32, name="state")
+                        cand[s] = gate_banks.tile([P, COLS], F32, name="cand")
+                    for w_name, a_name, acc, start, stop in (
+                        ("xr", "x", reset, True, False),
+                        ("hr", "h", reset, False, True),
+                        ("hh", "h", state, True, True),
+                        ("xh", "x", cand, True, True),
+                    ):
+                        for s in slices:
+                            nc.tensor.matmul_mx(
+                                out=acc[s][:],
+                                lhsT=w_codes[w_name][:, s * P : (s + 1) * P].bitcast(FP8X4),
+                                lhsT_scale=w_scales[w_name][:, s * P : (s + 1) * P],
+                                rhs=codes[a_name, half][:].bitcast(FP8X4),
+                                rhs_scale=scales[a_name, half][:],
+                                start=start,
+                                stop=stop,
+                            )
+
+                    gate = {}
+                    for s in slices:
+                        gate[s] = work.tile([P, COLS], F32, name="gate")
+                        nc.scalar.activation(
+                            out=gate[s][:], in_=reset[s][:], func=ACT.Sigmoid, bias=bias[:, s : s + 1]
+                        )
+                    gated = {}
+                    for s in slices:
+                        gated[s] = work.tile([P, COLS], F32, name="gated")
+                        nc.vector.tensor_tensor(out=gated[s][:], in0=state[s][:], in1=gate[s][:], op=ALU.mult)
+                    for s in slices:
+                        before_tanh[half, s] = work.tile([P, COLS], F32, name="before_tanh")
+                        nc.vector.scalar_tensor_tensor(
+                            out=before_tanh[half, s][:],
+                            in0=cand[s][:],
+                            scalar=bias[:, SLICES + s : SLICES + s + 1],
+                            in1=gated[s][:],
+                            op0=ALU.add,
+                            op1=ALU.add,
+                        )
+
+                if pair > 0:
+                    half = (pair - 1) // (SLICES // 2)
+                    slices = [2 * ((pair - 1) % (SLICES // 2)), 2 * ((pair - 1) % (SLICES // 2)) + 1]
+                    for s in slices:
+                        back = gate_banks.tile([P, HALF_ROWS, P], F32, name="back")
+                        for j in range(HALF_ROWS):
+                            nc.tensor.transpose(back[:, j, :], before_tanh[half, s][:, j * P : (j + 1) * P], ident[:])
+                        result = work.tile([P, HALF_ROWS, P], F32, name="result")
+                        nc.scalar.activation(out=result[:], in_=back[:], func=ACT.Tanh)
+                        nc.sync.dma_start(
+                            out=out_rows[:, half * HALF_ROWS : (half + 1) * HALF_ROWS, s * P : (s + 1) * P],
+                            in_=result[:],
+                        )
+
+
+def quantise(nc, keep, key, grouped, codes, scales):
+    codes[key] = keep.tile([P, COLS], U32, name="codes_%s%d" % key, align_bytes=64)
+    scales[key] = keep.tile([P, COLS], U8, name="scales_%s%d" % key, align_bytes=64)
+    nc.vector.quantize_mx(out=codes[key][:].bitcast(FP8X4), scales=scales[key][:], in_=grouped[key][:])

@@ -113,9 +113,6 @@ def tile_augru_pa_kernel(
         with tc.psum_pool(name="front_banks", bufs=8) as front_banks:
             bias_rows_f32 = keep.tile([P, P], F32)
             nc.vector.tensor_copy(out=bias_rows_f32[:], in_=bias_rows[:])
-            bank = front_banks.tile([P, 2, 2, P], F32)
-            nc.tensor.transpose(bank[:, 0, 0, :], bias_rows_f32[:], ident[:])
-            nc.vector.tensor_copy(out=bias[:], in_=bank[:, 0, 0, 0 : 2 * SLICES])
 
             waiting = None
             for half in range(HALVES):
@@ -140,6 +137,9 @@ def tile_augru_pa_kernel(
                     if waiting is not None:
                         quantise(nc, keep, waiting, grouped, codes, scales)
                     waiting = (name, half)
+            bank = front_banks.tile([P, 2, 2, P], F32)
+            nc.tensor.transpose(bank[:, 0, 0, :], bias_rows_f32[:], ident[:])
+            nc.vector.tensor_copy(out=bias[:], in_=bank[:, 0, 0, 0 : 2 * SLICES])
             quantise(nc, keep, waiting, grouped, codes, scales)
 
         with tc.psum_pool(name="gate_banks", bufs=2, reuse_waits="tile") as gate_banks:

@@ -142,6 +142,17 @@ def tile_augru_pa_kernel(
             nc.vector.tensor_copy(out=bias[:], in_=bank[:, 0, 0, 0 : 2 * SLICES])
             quantise(nc, keep, waiting, grouped, codes, scales)
 
+        def mx_pass(acc, w_name, a_name, half, s, start, stop):
+            nc.tensor.matmul_mx(
+                out=acc[:],
+                lhsT=w_codes[w_name][:, s * P : (s + 1) * P].bitcast(FP8X4),
+                lhsT_scale=w_scales[w_name][:, s * P : (s + 1) * P],
+                rhs=codes[a_name, half][:].bitcast(FP8X4),
+                rhs_scale=scales[a_name, half][:],
+                start=start,
+                stop=stop,
+            )
+
         with tc.psum_pool(name="gate_banks", bufs=2, reuse_waits="tile") as gate_banks:
             before_tanh = {}
             for pair in range(PAIRS + 1):
@@ -156,22 +167,13 @@ def tile_augru_pa_kernel(
                         reset[s] = gate_banks.tile([P, COLS], F32, name="reset")
                         state[s] = gate_banks.tile([P, COLS], F32, name="state")
                         cand[s] = gate_banks.tile([P, COLS], F32, name="cand")
-                    for w_name, a_name, acc, start, stop in (
-                        ("xr", "x", reset, True, False),
-                        ("hr", "h", reset, False, True),
-                        ("hh", "h", state, True, True),
-                        ("xh", "x", cand, True, True),
-                    ):
-                        for s in slices:
-                            nc.tensor.matmul_mx(
-                                out=acc[s][:],
-                                lhsT=w_codes[w_name][:, s * P : (s + 1) * P].bitcast(FP8X4),
-                                lhsT_scale=w_scales[w_name][:, s * P : (s + 1) * P],
-                                rhs=codes[a_name, half][:].bitcast(FP8X4),
-                                rhs_scale=scales[a_name, half][:],
-                                start=start,
-                                stop=stop,
-                            )
+                    for s in slices:
+                        mx_pass(reset[s], "xr", "x", half, s, True, False)
+                        mx_pass(reset[s], "hr", "h", half, s, False, True)
+                    for s in slices:
+                        mx_pass(state[s], "hh", "h", half, s, True, True)
+                    for s in slices:
+                        mx_pass(cand[s], "xh", "x", half, s, True, True)
 
                     gate = {}
                     for s in slices:
@@ -202,11 +204,16 @@ def tile_augru_pa_kernel(
                         for j in range(HALF_ROWS):
                             nc.tensor.transpose(back[:, j, :], before_tanh[half, s][:, j * P : (j + 1) * P], ident[:])
                         result = work.tile([P, HALF_ROWS, P], F32, name="result")
-                        nc.scalar.activation(out=result[:], in_=back[:], func=ACT.Tanh)
-                        nc.sync.dma_start(
-                            out=out_rows[:, half * HALF_ROWS : (half + 1) * HALF_ROWS, s * P : (s + 1) * P],
-                            in_=result[:],
-                        )
+                        for first in range(0, HALF_ROWS, 2):
+                            nc.scalar.activation(
+                                out=result[:, first : first + 2, :], in_=back[:, first : first + 2, :], func=ACT.Tanh
+                            )
+                            nc.sync.dma_start(
+                                out=out_rows[
+                                    :, half * HALF_ROWS + first : half * HALF_ROWS + first + 2, s * P : (s + 1) * P
+                                ],
+                                in_=result[:, first : first + 2, :],
+                            )
 
 
 def quantise(nc, keep, key, grouped, codes, scales):

@@ -23,6 +23,8 @@ HALF_ROWS = ROWS // HALVES
 COLS = HALF_ROWS * P
 SLICES = UNITS // P
 PAIRS = HALVES * SLICES // 2
+WARM_UP = 4
+WARM_BETWEEN = 2
 
 FLOPS = 2 * 4 * BATCH * FEATURES * UNITS
 
@@ -60,6 +62,9 @@ def tile_augru_pa_kernel(
 
         ident = keep.tile([P, P], F32)
         make_identity(nc, ident[:])
+
+        zeros = keep.tile([P, COLS], BF16)
+        nc.vector.memset(zeros[:], 0.0)
 
         bias_rows = keep.tile([P, P], BF16)
         nc.vector.memset(bias_rows[:], 0.0)
@@ -114,6 +119,19 @@ def tile_augru_pa_kernel(
             bias_rows_f32 = keep.tile([P, P], F32)
             nc.vector.tensor_copy(out=bias_rows_f32[:], in_=bias_rows[:])
 
+            def keep_warm(count):
+                bank = front_banks.tile([P, 2, 2, P], F32)
+                for repeat in range(count):
+                    nc.tensor.matmul(
+                        out=bank[:].rearrange("p j u b -> p (j u b)"),
+                        lhsT=zeros[:, 0:P],
+                        rhs=zeros[:],
+                        start=True,
+                        stop=True,
+                    )
+
+            keep_warm(WARM_UP)
+
             waiting = None
             for half in range(HALVES):
                 for name in ("x", "h"):
@@ -134,6 +152,7 @@ def tile_augru_pa_kernel(
                             out=pairs_out[:, first : first + 2],
                             in_=bank[:].rearrange("p j u b -> p j b u"),
                         )
+                    keep_warm(WARM_BETWEEN)
                     if waiting is not None:
                         quantise(nc, keep, waiting, grouped, codes, scales)
                     waiting = (name, half)

@@ -59,6 +59,7 @@ def tile_augru_pa_kernel(
         ctx.enter_context(tc.manual_schedule())
         keep = ctx.enter_context(tc.tile_pool(name="keep", bufs=1))
         work = ctx.enter_context(tc.tile_pool(name="work", bufs=4))
+        banks = ctx.enter_context(tc.psum_pool(name="banks", bufs=8))
 
         ident = keep.tile([P, P], F32)
         make_identity(nc, ident[:])
@@ -96,7 +97,7 @@ def tile_augru_pa_kernel(
             for r in range(4):
                 queue.dma_start(out=w_scales[name][r:P:32, :].bitcast(word), in_=by_r[r].bitcast(word))
 
-        for name in weights:
+        for name in ("xh", "xr", "hr", "hh"):
             w_scales[name] = keep.tile([P, UNITS], U8, name="w_scales_" + name, align_bytes=64)
             nc.vector.memset(w_scales[name][:].bitcast(I32), 0)
 
@@ -106,21 +107,21 @@ def tile_augru_pa_kernel(
         load_rows("x", 1)
         load_rows("h", 1)
         load_scales("hr", nc.sync, I32)
-        load_scales("hh", nc.gpsimd, F32)
+        load_scales("xh", nc.gpsimd, F32)
         for name in weights:
             load_codes(name)
-        load_scales("xh", nc.sync, I32)
+        load_scales("hh", nc.sync, I32)
 
         codes = {}
         scales = {}
         grouped = {}
         bias = keep.tile([P, 2 * SLICES], F32)
-        with tc.psum_pool(name="front_banks", bufs=8) as front_banks:
+        if True:
             bias_rows_f32 = keep.tile([P, P], F32)
             nc.vector.tensor_copy(out=bias_rows_f32[:], in_=bias_rows[:])
 
             def keep_warm(count):
-                bank = front_banks.tile([P, 2, 2, P], F32)
+                bank = banks.tile([P, 2, 2, P], F32, name="bank")
                 for repeat in range(count):
                     nc.tensor.matmul(
                         out=bank[:].rearrange("p j u b -> p (j u b)"),
@@ -142,7 +143,7 @@ def tile_augru_pa_kernel(
                         "p (j b u) -> p j b u", j=HALF_ROWS, u=2
                     )
                     for first in range(0, HALF_ROWS, 2):
-                        bank = front_banks.tile([P, 2, 2, P], F32)
+                        bank = banks.tile([P, 2, 2, P], F32, name="bank")
                         for j in range(2):
                             pairs_in = raw[name, half][:, first + j, :].bitcast(F32)
                             for u in range(2):
@@ -152,11 +153,12 @@ def tile_augru_pa_kernel(
                             out=pairs_out[:, first : first + 2],
                             in_=bank[:].rearrange("p j u b -> p j b u"),
                         )
-                    keep_warm(WARM_BETWEEN)
+                    if (name, half) != ("h", HALVES - 1):
+                        keep_warm(WARM_BETWEEN)
                     if waiting is not None:
                         quantise(nc, keep, waiting, grouped, codes, scales)
                     waiting = (name, half)
-            bank = front_banks.tile([P, 2, 2, P], F32)
+            bank = banks.tile([P, 2, 2, P], F32, name="bank")
             nc.tensor.transpose(bank[:, 0, 0, :], bias_rows_f32[:], ident[:])
             nc.vector.tensor_copy(out=bias[:], in_=bank[:, 0, 0, 0 : 2 * SLICES])
             quantise(nc, keep, waiting, grouped, codes, scales)
@@ -172,7 +174,7 @@ def tile_augru_pa_kernel(
                 stop=stop,
             )
 
-        with tc.psum_pool(name="gate_banks", bufs=2, reuse_waits="tile") as gate_banks:
+        if True:
             before_tanh = {}
             for pair in range(PAIRS + 1):
                 if pair < PAIRS:
@@ -183,9 +185,9 @@ def tile_augru_pa_kernel(
                     state = {}
                     cand = {}
                     for s in slices:
-                        reset[s] = gate_banks.tile([P, COLS], F32, name="reset")
-                        state[s] = gate_banks.tile([P, COLS], F32, name="state")
-                        cand[s] = gate_banks.tile([P, COLS], F32, name="cand")
+                        reset[s] = banks.tile([P, COLS], F32, name="bank")
+                        state[s] = banks.tile([P, COLS], F32, name="bank")
+                        cand[s] = banks.tile([P, COLS], F32, name="bank")
                     for s in slices:
                         mx_pass(reset[s], "xr", "x", half, s, True, False)
                         mx_pass(reset[s], "hr", "h", half, s, False, True)
@@ -219,7 +221,7 @@ def tile_augru_pa_kernel(
                     half = (pair - 1) // (SLICES // 2)
                     slices = [2 * ((pair - 1) % (SLICES // 2)), 2 * ((pair - 1) % (SLICES // 2)) + 1]
                     for s in slices:
-                        back = gate_banks.tile([P, HALF_ROWS, P], F32, name="back")
+                        back = banks.tile([P, HALF_ROWS, P], F32, name="bank")
                         for j in range(HALF_ROWS):
                             nc.tensor.transpose(back[:, j, :], before_tanh[half, s][:, j * P : (j + 1) * P], ident[:])
                         result = work.tile([P, HALF_ROWS, P], F32, name="result")

@@ -61,111 +61,118 @@ def tile_augru_pa_kernel(
         work = ctx.enter_context(tc.tile_pool(name="work", bufs=4))
         banks = ctx.enter_context(tc.psum_pool(name="banks", bufs=8))
 
-        ident = keep.tile([P, P], F32)
+        def new_bank():
+            bank = banks.tile([P, COLS], F32, name="bank")
+            return bank
+
+        raw, sorted_words, grouped, codes, scales = {}, {}, {}, {}, {}
+        units = [(name, half) for half in range(HALVES) for name in ("x", "h")]
+        for key in units:
+            raw[key] = keep.tile([P, HALF_ROWS, FEATURES], BF16, name="raw_%s%d" % key)
+            sorted_words[key] = keep.tile([P, HALF_ROWS, 2, P], F32, name="sorted_%s%d" % key)
+            grouped[key] = keep.tile([P, COLS * PACK], BF16, name="grouped_%s%d" % key, align_bytes=64)
+            codes[key] = keep.tile([P, COLS], U32, name="codes_%s%d" % key, align_bytes=64)
+            scales[key] = keep.tile([P, COLS], U8, name="scales_%s%d" % key, align_bytes=64)
+        w_codes, w_scales = {}, {}
+        for name in weights:
+            w_codes[name] = keep.tile([P, UNITS], U32, name="w_codes_" + name, align_bytes=64)
+            w_scales[name] = keep.tile([P, UNITS], U8, name="w_scales_" + name, align_bytes=64)
+        ident = keep.tile([P, P], F32, name="ident")
+        bias_rows = keep.tile([P, P], BF16, name="bias_rows")
+        pick = keep.tile([P, 2 * SLICES], BF16, name="pick")
+        bias = keep.tile([P, 2 * SLICES], F32, name="bias")
+        zeros = keep.tile([P, COLS], BF16, name="zeros")
+        warm = keep.tile([P, 2], F32, name="warm")
+
         make_identity(nc, ident[:])
-
-        zeros = keep.tile([P, COLS], BF16)
         nc.vector.memset(zeros[:], 0.0)
-
-        bias_rows = keep.tile([P, P], BF16)
         nc.vector.memset(bias_rows[:], 0.0)
         nc.scalar.dma_start(out=bias_rows[0:SLICES, :], in_=b_r.rearrange("(s u) -> s u", u=P))
         nc.scalar.dma_start(out=bias_rows[SLICES : 2 * SLICES, :], in_=b_h.rearrange("(s u) -> s u", u=P))
-
-        warm = keep.tile([P, 2], F32)
         nc.vector.memset(warm[:], 0.0)
+        for name in ("hh", "xr", "hr", "xh"):
+            nc.vector.memset(w_scales[name][:].bitcast(I32), 0)
         nc.scalar.activation(out=warm[:, 1:2], in_=warm[:, 0:1], func=ACT.Sigmoid)
-
-        raw = {}
-        w_codes = {}
-        w_scales = {}
+        nc.vector.tensor_copy(out=pick[:], in_=ident[:, 0 : 2 * SLICES])
 
         def load_rows(name, half):
             rows = activations[name].rearrange("(p j) k -> p j k", j=ROWS)
-            raw[name, half] = keep.tile([P, HALF_ROWS, FEATURES], BF16, name="raw_%s%d" % (name, half))
             nc.sync.dma_start(out=raw[name, half][:], in_=rows[:, half * HALF_ROWS : (half + 1) * HALF_ROWS, :])
 
         def load_codes(name):
-            w_codes[name] = keep.tile([P, UNITS], U32, name="w_codes_" + name, align_bytes=64)
             nc.sync.dma_start(
                 out=w_codes[name][:].bitcast(I32),
                 in_=weights[name][0].rearrange("g p n t -> (g p) (n t)").bitcast(I32),
             )
 
-        def load_scales(name, queue, word):
+        def load_scales(name, queue, word, rows=(0, 1, 2, 3)):
             by_r = weights[name][1].rearrange("g (q r) n -> (g r) q n", r=4)
-            for r in range(4):
+            for r in rows:
                 queue.dma_start(out=w_scales[name][r:P:32, :].bitcast(word), in_=by_r[r].bitcast(word))
-
-        for name in ("xh", "xr", "hr", "hh"):
-            w_scales[name] = keep.tile([P, UNITS], U8, name="w_scales_" + name, align_bytes=64)
-            nc.vector.memset(w_scales[name][:].bitcast(I32), 0)
 
         load_rows("x", 0)
         load_rows("h", 0)
-        load_scales("xr", nc.sync, I32)
+        load_scales("xr", nc.sync, I32, (0, 1, 2, 3,))
         load_rows("x", 1)
         load_rows("h", 1)
-        load_scales("hr", nc.sync, I32)
-        load_scales("xh", nc.gpsimd, F32)
-        for name in weights:
-            load_codes(name)
-        load_scales("hh", nc.sync, I32)
+        load_scales("hr", nc.sync, I32, (0, 1, 2, 3,))
+        load_scales("hh", nc.gpsimd, F32)
+        load_codes("xr")
+        load_codes("hr")
+        load_codes("hh")
+        load_codes("xh")
+        load_scales("xh", nc.sync, I32, (0, 1, 2, 3,))
 
-        codes = {}
-        scales = {}
-        grouped = {}
-        bias = keep.tile([P, 2 * SLICES], F32)
-        if True:
-            bias_rows_f32 = keep.tile([P, P], F32)
-            nc.vector.tensor_copy(out=bias_rows_f32[:], in_=bias_rows[:])
+        def keep_warm(count):
+            bank = new_bank()
+            for repeat in range(count):
+                nc.tensor.matmul(out=bank[:], lhsT=zeros[:, 0:P], rhs=zeros[:], start=True, stop=True)
 
-            def keep_warm(count):
-                bank = banks.tile([P, 2, 2, P], F32, name="bank")
-                for repeat in range(count):
-                    nc.tensor.matmul(
-                        out=bank[:].rearrange("p j u b -> p (j u b)"),
-                        lhsT=zeros[:, 0:P],
-                        rhs=zeros[:],
-                        start=True,
-                        stop=True,
-                    )
+        sorted_keys = []
 
-            keep_warm(WARM_UP)
+        def sort_words(key):
+            sorted_keys.append(key)
+            nc.vector.tensor_copy(
+                out=sorted_words[key][:], in_=raw[key][:].bitcast(F32).rearrange("p j (w u) -> p j u w", u=2)
+            )
 
-            waiting = None
-            for half in range(HALVES):
-                for name in ("x", "h"):
-                    grouped[name, half] = keep.tile(
-                        [P, COLS * PACK], BF16, name="grouped_%s%d" % (name, half), align_bytes=64
-                    )
-                    pairs_out = grouped[name, half][:].bitcast(F32).rearrange(
-                        "p (j b u) -> p j b u", j=HALF_ROWS, u=2
-                    )
-                    for first in range(0, HALF_ROWS, 2):
-                        bank = banks.tile([P, 2, 2, P], F32, name="bank")
-                        for j in range(2):
-                            pairs_in = raw[name, half][:, first + j, :].bitcast(F32)
-                            for u in range(2):
-                                nc.tensor.transpose(bank[:, j, u, :], pairs_in[:, u : FEATURES // 2 : 2], ident[:])
-                        copy_out = nc.vector.tensor_copy if first == 0 else nc.scalar.copy
-                        copy_out(
-                            out=pairs_out[:, first : first + 2],
-                            in_=bank[:].rearrange("p j u b -> p j b u"),
-                        )
-                    if (name, half) != ("h", HALVES - 1):
-                        keep_warm(WARM_BETWEEN)
-                    if waiting is not None:
-                        quantise(nc, keep, waiting, grouped, codes, scales)
-                    waiting = (name, half)
-            bank = banks.tile([P, 2, 2, P], F32, name="bank")
-            nc.tensor.transpose(bank[:, 0, 0, :], bias_rows_f32[:], ident[:])
-            nc.vector.tensor_copy(out=bias[:], in_=bank[:, 0, 0, 0 : 2 * SLICES])
-            quantise(nc, keep, waiting, grouped, codes, scales)
+        turned = {}
 
-        def mx_pass(acc, w_name, a_name, half, s, start, stop):
+        def turn(key):
+            for first in range(0, HALF_ROWS, 2):
+                bank = new_bank()
+                by_set = bank[:].rearrange("p (j u b) -> p j u b", j=2, u=2)
+                for j in range(2):
+                    for u in range(2):
+                        if key in sorted_keys:
+                            words = sorted_words[key][:, first + j, u, :]
+                        else:
+                            words = raw[key][:, first + j, :].bitcast(F32)[:, u : FEATURES // 2 : 2]
+                        nc.tensor.transpose(by_set[:, j, u, :], words, ident[:])
+                turned[key, first] = bank
+
+        def empty(key, first, copy_out):
+            pairs_out = grouped[key][:].bitcast(F32).rearrange("p (j b u) -> p j b u", j=HALF_ROWS, u=2)
+            copy_out(
+                out=pairs_out[:, first : first + 2],
+                in_=turned[key, first][:].rearrange("p (j u b) -> p j b u", j=2, u=2),
+            )
+
+        def quantise(key):
+            nc.vector.quantize_mx(out=codes[key][:].bitcast(FP8X4), scales=scales[key][:], in_=grouped[key][:])
+
+        def bias_columns():
+            bank = new_bank()
+            nc.tensor.matmul(out=bank[:, 0 : 2 * SLICES], lhsT=bias_rows[:], rhs=pick[:], start=True, stop=True)
+            nc.scalar.copy(out=bias[:], in_=bank[:, 0 : 2 * SLICES])
+
+        acc, gate, gated, before_tanh = {}, {}, {}, {}
+        sum_of = {"xr": "reset", "hr": "reset", "hh": "state", "xh": "cand"}
+
+        def mx_pass(w_name, half, s, start, stop):
+            a_name = w_name[0]
             nc.tensor.matmul_mx(
-                out=acc[:],
+                out=acc[sum_of[w_name], half, s][:],
                 lhsT=w_codes[w_name][:, s * P : (s + 1) * P].bitcast(FP8X4),
                 lhsT_scale=w_scales[w_name][:, s * P : (s + 1) * P],
                 rhs=codes[a_name, half][:].bitcast(FP8X4),
@@ -174,70 +181,105 @@ def tile_augru_pa_kernel(
                 stop=stop,
             )
 
-        if True:
-            before_tanh = {}
-            for pair in range(PAIRS + 1):
-                if pair < PAIRS:
-                    half = pair // (SLICES // 2)
-                    slices = [2 * (pair % (SLICES // 2)), 2 * (pair % (SLICES // 2)) + 1]
+        def passes(half, slices):
+            for s in slices:
+                for kind in ("reset", "state", "cand"):
+                    acc[kind, half, s] = new_bank()
+            for s in slices:
+                mx_pass("xr", half, s, True, False)
+                mx_pass("hr", half, s, False, True)
+            for s in slices:
+                mx_pass("hh", half, s, True, True)
+            for s in slices:
+                mx_pass("xh", half, s, True, True)
 
-                    reset = {}
-                    state = {}
-                    cand = {}
-                    for s in slices:
-                        reset[s] = banks.tile([P, COLS], F32, name="bank")
-                        state[s] = banks.tile([P, COLS], F32, name="bank")
-                        cand[s] = banks.tile([P, COLS], F32, name="bank")
-                    for s in slices:
-                        mx_pass(reset[s], "xr", "x", half, s, True, False)
-                        mx_pass(reset[s], "hr", "h", half, s, False, True)
-                    for s in slices:
-                        mx_pass(state[s], "hh", "h", half, s, True, True)
-                    for s in slices:
-                        mx_pass(cand[s], "xh", "x", half, s, True, True)
+        def sigmoid(half, s):
+            gate[half, s] = work.tile([P, COLS], F32, name="gate")
+            nc.scalar.activation(
+                out=gate[half, s][:], in_=acc["reset", half, s][:], func=ACT.Sigmoid, bias=bias[:, s : s + 1]
+            )
 
-                    gate = {}
-                    for s in slices:
-                        gate[s] = work.tile([P, COLS], F32, name="gate")
-                        nc.scalar.activation(
-                            out=gate[s][:], in_=reset[s][:], func=ACT.Sigmoid, bias=bias[:, s : s + 1]
-                        )
-                    gated = {}
-                    for s in slices:
-                        gated[s] = work.tile([P, COLS], F32, name="gated")
-                        nc.vector.tensor_tensor(out=gated[s][:], in0=state[s][:], in1=gate[s][:], op=ALU.mult)
-                    for s in slices:
-                        before_tanh[half, s] = work.tile([P, COLS], F32, name="before_tanh")
-                        nc.vector.scalar_tensor_tensor(
-                            out=before_tanh[half, s][:],
-                            in0=cand[s][:],
-                            scalar=bias[:, SLICES + s : SLICES + s + 1],
-                            in1=gated[s][:],
-                            op0=ALU.add,
-                            op1=ALU.add,
-                        )
+        def multiply(half, s):
+            gated[half, s] = work.tile([P, COLS], F32, name="gated")
+            nc.vector.tensor_tensor(
+                out=gated[half, s][:], in0=acc["state", half, s][:], in1=gate[half, s][:], op=ALU.mult
+            )
 
-                if pair > 0:
-                    half = (pair - 1) // (SLICES // 2)
-                    slices = [2 * ((pair - 1) % (SLICES // 2)), 2 * ((pair - 1) % (SLICES // 2)) + 1]
-                    for s in slices:
-                        back = banks.tile([P, HALF_ROWS, P], F32, name="bank")
-                        for j in range(HALF_ROWS):
-                            nc.tensor.transpose(back[:, j, :], before_tanh[half, s][:, j * P : (j + 1) * P], ident[:])
-                        result = work.tile([P, HALF_ROWS, P], F32, name="result")
-                        for first in range(0, HALF_ROWS, 2):
-                            nc.scalar.activation(
-                                out=result[:, first : first + 2, :], in_=back[:, first : first + 2, :], func=ACT.Tanh
-                            )
-                            nc.sync.dma_start(
-                                out=out_rows[
-                                    :, half * HALF_ROWS + first : half * HALF_ROWS + first + 2, s * P : (s + 1) * P
-                                ],
-                                in_=result[:, first : first + 2, :],
-                            )
+        def add(half, s):
+            before_tanh[half, s] = work.tile([P, COLS], F32, name="before_tanh")
+            nc.vector.scalar_tensor_tensor(
+                out=before_tanh[half, s][:],
+                in0=acc["cand", half, s][:],
+                scalar=bias[:, SLICES + s : SLICES + s + 1],
+                in1=gated[half, s][:],
+                op0=ALU.add,
+                op1=ALU.add,
+            )
 
+        def back(half, s):
+            bank = new_bank()
+            by_set = bank[:].rearrange("p (j u) -> p j u", j=HALF_ROWS)
+            for j in range(HALF_ROWS):
+                nc.tensor.transpose(by_set[:, j, :], before_tanh[half, s][:, j * P : (j + 1) * P], ident[:])
+            result = work.tile([P, HALF_ROWS, P], F32, name="result")
+            for first in range(0, HALF_ROWS, 2):
+                nc.scalar.activation(
+                    out=result[:, first : first + 2, :], in_=by_set[:, first : first + 2, :], func=ACT.Tanh
+                )
+                row = half * HALF_ROWS + first
+                nc.sync.dma_start(out=out_rows[:, row : row + 2, s * P : (s + 1) * P], in_=result[:, first : first + 2, :])
 
-def quantise(nc, keep, key, grouped, codes, scales):
-    codes[key] = keep.tile([P, COLS], U32, name="codes_%s%d" % key, align_bytes=64)
-    scales[key] = keep.tile([P, COLS], U8, name="scales_%s%d" % key, align_bytes=64)
-    nc.vector.quantize_mx(out=codes[key][:].bitcast(FP8X4), scales=scales[key][:], in_=grouped[key][:])
+        x0, h0, x1, h1 = units
+        V, S = nc.vector.tensor_copy, nc.scalar.copy
+        low, high = [0, 1], [2, 3]
+        keep_warm(WARM_UP)
+        turn(x0)
+        keep_warm(WARM_BETWEEN)
+        empty(x0, 0, V)
+        empty(x0, 2, S)
+        turn(h0)
+        keep_warm(WARM_BETWEEN)
+        bias_columns()
+        empty(h0, 0, V)
+        empty(h0, 2, S)
+        sort_words(x1)
+        quantise(x0)
+        turn(x1)
+        keep_warm(WARM_BETWEEN)
+        empty(x1, 0, S)
+        empty(x1, 2, S)
+        sort_words(h1)
+        quantise(h0)
+        turn(h1)
+        empty(h1, 0, S)
+        empty(h1, 2, V)
+        quantise(x1)
+        passes(0, low)
+        for s in low:
+            sigmoid(0, s)
+        for s in low:
+            multiply(0, s)
+        for s in low:
+            add(0, s)
+        quantise(h1)
+        passes(0, high)
+        for s in high:
+            sigmoid(0, s)
+        for s in high:
+            multiply(0, s)
+        for s in high:
+            add(0, s)
+        for s in low:
+            back(0, s)
+        for half, slices, last_half, last_slices in ((1, low, 0, high), (1, high, 1, low)):
+            passes(half, slices)
+            for s in slices:
+                sigmoid(half, s)
+            for s in slices:
+                multiply(half, s)
+            for s in slices:
+                add(half, s)
+            for s in last_slices:
+                back(last_half, s)
+        for s in high:
+            back(1, s)

@@ -23,7 +23,7 @@ HALF_ROWS = ROWS // HALVES
 COLS = HALF_ROWS * P
 SLICES = UNITS // P
 PAIRS = HALVES * SLICES // 2
-WARM_UP = 4
+WARM_UP = 6
 WARM_BETWEEN = 2
 
 FLOPS = 2 * 4 * BATCH * FEATURES * UNITS

@@ -23,7 +23,7 @@ HALF_ROWS = ROWS // HALVES
 COLS = HALF_ROWS * P
 SLICES = UNITS // P
 PAIRS = HALVES * SLICES // 2
-WARM_UP = 6
+WARM_UP = 4
 WARM_BETWEEN = 2
 
 FLOPS = 2 * 4 * BATCH * FEATURES * UNITS
@@ -237,19 +237,19 @@ def tile_augru_pa_kernel(
         keep_warm(WARM_BETWEEN)
         empty(x0, 0, V)
         empty(x0, 2, S)
+        bias_columns()
         turn(h0)
         keep_warm(WARM_BETWEEN)
-        bias_columns()
-        empty(h0, 0, V)
+        empty(h0, 0, S)
         empty(h0, 2, S)
-        sort_words(x1)
         quantise(x0)
+        sort_words(x1)
         turn(x1)
-        keep_warm(WARM_BETWEEN)
+        keep_warm(1)
         empty(x1, 0, S)
-        empty(x1, 2, S)
         sort_words(h1)
         quantise(h0)
+        empty(x1, 2, V)
         turn(h1)
         empty(h1, 0, S)
         empty(h1, 2, V)

@@ -85,12 +85,14 @@ def tile_augru_pa_kernel(
         warm = keep.tile([P, 2], F32, name="warm")
 
         make_identity(nc, ident[:])
-        nc.vector.memset(zeros[:], 0.0)
         nc.vector.memset(bias_rows[:], 0.0)
         nc.scalar.dma_start(out=bias_rows[0:SLICES, :], in_=b_r.rearrange("(s u) -> s u", u=P))
         nc.scalar.dma_start(out=bias_rows[SLICES : 2 * SLICES, :], in_=b_h.rearrange("(s u) -> s u", u=P))
+        for name in ("xr", "hh"):
+            nc.vector.memset(w_scales[name][:].bitcast(I32), 0)
+        nc.vector.memset(zeros[:], 0.0)
         nc.vector.memset(warm[:], 0.0)
-        for name in ("hh", "xr", "hr", "xh"):
+        for name in ("hr", "xh"):
             nc.vector.memset(w_scales[name][:].bitcast(I32), 0)
         nc.scalar.activation(out=warm[:, 1:2], in_=warm[:, 0:1], func=ACT.Sigmoid)
         nc.vector.tensor_copy(out=pick[:], in_=ident[:, 0 : 2 * SLICES])
@@ -112,16 +114,19 @@ def tile_augru_pa_kernel(
 
         load_rows("x", 0)
         load_rows("h", 0)
-        load_scales("xr", nc.sync, I32, (0, 1, 2, 3,))
+        load_scales("xr", nc.sync, I32, (0, 1))
         load_rows("x", 1)
         load_rows("h", 1)
-        load_scales("hr", nc.sync, I32, (0, 1, 2, 3,))
-        load_scales("hh", nc.gpsimd, F32)
+        load_scales("hr", nc.sync, I32, (0, 1))
         load_codes("xr")
         load_codes("hr")
+        load_scales("hr", nc.sync, I32, (2, 3))
         load_codes("hh")
         load_codes("xh")
-        load_scales("xh", nc.sync, I32, (0, 1, 2, 3,))
+        load_scales("hh", nc.sync, I32, (2, 3))
+        load_scales("xh", nc.sync, I32)
+        load_scales("xr", nc.gpsimd, F32, (2, 3))
+        load_scales("hh", nc.gpsimd, F32, (0, 1))
 
         def keep_warm(count):
             bank = new_bank()
@@ -242,8 +247,8 @@ def tile_augru_pa_kernel(
         keep_warm(WARM_BETWEEN)
         empty(h0, 0, S)
         empty(h0, 2, S)
-        quantise(x0)
         sort_words(x1)
+        quantise(x0)
         turn(x1)
         keep_warm(1)
         empty(x1, 0, S)

@@ -58,7 +58,7 @@ def tile_augru_pa_kernel(
     with ExitStack() as ctx:
         ctx.enter_context(tc.manual_schedule())
         keep = ctx.enter_context(tc.tile_pool(name="keep", bufs=1))
-        work = ctx.enter_context(tc.tile_pool(name="work", bufs=4))
+        work = ctx.enter_context(tc.tile_pool(name="work", bufs=8))
         banks = ctx.enter_context(tc.psum_pool(name="banks", bufs=8))
 
         def new_bank():
@@ -186,17 +186,30 @@ def tile_augru_pa_kernel(
                 stop=stop,
             )
 
-        def passes(half, slices):
+        def open_banks(kind, half, slices):
             for s in slices:
-                for kind in ("reset", "state", "cand"):
-                    acc[kind, half, s] = new_bank()
+                acc[kind, half, s] = new_bank()
+
+        def reset_passes(half, slices):
+            open_banks("reset", half, slices)
             for s in slices:
                 mx_pass("xr", half, s, True, False)
                 mx_pass("hr", half, s, False, True)
+
+        def state_passes(half, slices):
+            open_banks("state", half, slices)
             for s in slices:
                 mx_pass("hh", half, s, True, True)
+
+        def candidate_passes(half, slices):
+            open_banks("cand", half, slices)
             for s in slices:
                 mx_pass("xh", half, s, True, True)
+
+        def passes(half, slices):
+            reset_passes(half, slices)
+            state_passes(half, slices)
+            candidate_passes(half, slices)
 
         def sigmoid(half, s):
             gate[half, s] = work.tile([P, COLS], F32, name="gate")
@@ -221,18 +234,21 @@ def tile_augru_pa_kernel(
                 op1=ALU.add,
             )
 
-        def back(half, s):
+        def back(half, s, steps):
             bank = new_bank()
             by_set = bank[:].rearrange("p (j u) -> p j u", j=HALF_ROWS)
             for j in range(HALF_ROWS):
                 nc.tensor.transpose(by_set[:, j, :], before_tanh[half, s][:, j * P : (j + 1) * P], ident[:])
             result = work.tile([P, HALF_ROWS, P], F32, name="result")
-            for first in range(0, HALF_ROWS, 2):
+            width = HALF_ROWS // steps
+            for first in range(0, HALF_ROWS, width):
                 nc.scalar.activation(
-                    out=result[:, first : first + 2, :], in_=by_set[:, first : first + 2, :], func=ACT.Tanh
+                    out=result[:, first : first + width, :], in_=by_set[:, first : first + width, :], func=ACT.Tanh
                 )
                 row = half * HALF_ROWS + first
-                nc.sync.dma_start(out=out_rows[:, row : row + 2, s * P : (s + 1) * P], in_=result[:, first : first + 2, :])
+                nc.sync.dma_start(
+                    out=out_rows[:, row : row + width, s * P : (s + 1) * P], in_=result[:, first : first + width, :]
+                )
 
         x0, h0, x1, h1 = units
         V, S = nc.vector.tensor_copy, nc.scalar.copy
@@ -259,32 +275,42 @@ def tile_augru_pa_kernel(
         empty(h1, 0, S)
         empty(h1, 2, V)
         quantise(x1)
-        passes(0, low)
-        for s in low:
-            sigmoid(0, s)
-        for s in low:
-            multiply(0, s)
-        for s in low:
-            add(0, s)
-        quantise(h1)
-        passes(0, high)
-        for s in high:
-            sigmoid(0, s)
-        for s in high:
-            multiply(0, s)
-        for s in high:
-            add(0, s)
-        for s in low:
-            back(0, s)
-        for half, slices, last_half, last_slices in ((1, low, 0, high), (1, high, 1, low)):
-            passes(half, slices)
+        def gates(half, slices):
             for s in slices:
                 sigmoid(half, s)
+
+        def products(half, slices):
             for s in slices:
                 multiply(half, s)
+
+        def sums(half, slices):
             for s in slices:
                 add(half, s)
-            for s in last_slices:
-                back(last_half, s)
-        for s in high:
-            back(1, s)
+
+        passes(0, low)
+        gates(0, low)
+        products(0, low)
+        sums(0, low)
+        quantise(h1)
+        passes(0, high)
+        gates(0, high)
+        products(0, high)
+        sums(0, high)
+        back(0, 0, 1)
+        back(0, 1, 1)
+        passes(1, low)
+        gates(1, low)
+        products(1, low)
+        sums(1, low)
+        reset_passes(1, high)
+        gates(1, high)
+        state_passes(1, high)
+        products(1, high)
+        back(0, 2, 1)
+        back(0, 3, 1)
+        back(1, 0, 1)
+        candidate_passes(1, high)
+        sums(1, high)
+        back(1, 1, 1)
+        back(1, 2, 2)
+        back(1, 3, 2)

@@ -21,8 +21,9 @@ ROWS = BATCH // P
 HALVES = 2
 HALF_ROWS = ROWS // HALVES
 COLS = HALF_ROWS * P
+QUARTER_ROWS = 2
+QUARTER_COLS = QUARTER_ROWS * P
 SLICES = UNITS // P
-PAIRS = HALVES * SLICES // 2
 WARM_UP = 4
 WARM_BETWEEN = 2
 
@@ -174,85 +175,89 @@ def tile_augru_pa_kernel(
         acc, gate, gated, before_tanh = {}, {}, {}, {}
         sum_of = {"xr": "reset", "hr": "reset", "hh": "state", "xh": "cand"}
 
-        def mx_pass(w_name, half, s, start, stop):
+        def mx_pass(w_name, quarter, s, start, stop):
             a_name = w_name[0]
+            half, columns = quarter // 2, slice(quarter % 2 * QUARTER_COLS, (quarter % 2 + 1) * QUARTER_COLS)
             nc.tensor.matmul_mx(
-                out=acc[sum_of[w_name], half, s][:],
+                out=acc[sum_of[w_name], quarter, s // 2][:, s % 2, :],
                 lhsT=w_codes[w_name][:, s * P : (s + 1) * P].bitcast(FP8X4),
                 lhsT_scale=w_scales[w_name][:, s * P : (s + 1) * P],
-                rhs=codes[a_name, half][:].bitcast(FP8X4),
-                rhs_scale=scales[a_name, half][:],
+                rhs=codes[a_name, half][:, columns].bitcast(FP8X4),
+                rhs_scale=scales[a_name, half][:, columns],
                 start=start,
                 stop=stop,
             )
 
-        def open_banks(kind, half, slices):
-            for s in slices:
-                acc[kind, half, s] = new_bank()
+        def passes(quarter):
+            for kind in ("reset", "state", "cand"):
+                for pair in range(SLICES // 2):
+                    acc[kind, quarter, pair] = new_bank()[:].rearrange("p (i b) -> p i b", i=2)
+            for s in range(SLICES):
+                mx_pass("xr", quarter, s, True, False)
+                mx_pass("hr", quarter, s, False, True)
+            for s in range(SLICES):
+                mx_pass("hh", quarter, s, True, True)
+            for s in range(SLICES):
+                mx_pass("xh", quarter, s, True, True)
 
-        def reset_passes(half, slices):
-            open_banks("reset", half, slices)
-            for s in slices:
-                mx_pass("xr", half, s, True, False)
-                mx_pass("hr", half, s, False, True)
-
-        def state_passes(half, slices):
-            open_banks("state", half, slices)
-            for s in slices:
-                mx_pass("hh", half, s, True, True)
-
-        def candidate_passes(half, slices):
-            open_banks("cand", half, slices)
-            for s in slices:
-                mx_pass("xh", half, s, True, True)
-
-        def passes(half, slices):
-            reset_passes(half, slices)
-            state_passes(half, slices)
-            candidate_passes(half, slices)
-
-        def sigmoid(half, s):
-            gate[half, s] = work.tile([P, COLS], F32, name="gate")
-            nc.scalar.activation(
-                out=gate[half, s][:], in_=acc["reset", half, s][:], func=ACT.Sigmoid, bias=bias[:, s : s + 1]
-            )
-
-        def multiply(half, s):
-            gated[half, s] = work.tile([P, COLS], F32, name="gated")
-            nc.vector.tensor_tensor(
-                out=gated[half, s][:], in0=acc["state", half, s][:], in1=gate[half, s][:], op=ALU.mult
-            )
-
-        def add(half, s):
-            before_tanh[half, s] = work.tile([P, COLS], F32, name="before_tanh")
-            nc.vector.scalar_tensor_tensor(
-                out=before_tanh[half, s][:],
-                in0=acc["cand", half, s][:],
-                scalar=bias[:, SLICES + s : SLICES + s + 1],
-                in1=gated[half, s][:],
-                op0=ALU.add,
-                op1=ALU.add,
-            )
-
-        def back(half, s, steps):
-            bank = new_bank()
-            by_set = bank[:].rearrange("p (j u) -> p j u", j=HALF_ROWS)
-            for j in range(HALF_ROWS):
-                nc.tensor.transpose(by_set[:, j, :], before_tanh[half, s][:, j * P : (j + 1) * P], ident[:])
-            result = work.tile([P, HALF_ROWS, P], F32, name="result")
-            width = HALF_ROWS // steps
-            for first in range(0, HALF_ROWS, width):
+        def sigmoid(quarter, pair):
+            gate[quarter, pair] = work.tile([P, 2, QUARTER_COLS], F32, name="gate")
+            for i in range(2):
+                s = 2 * pair + i
                 nc.scalar.activation(
-                    out=result[:, first : first + width, :], in_=by_set[:, first : first + width, :], func=ACT.Tanh
+                    out=gate[quarter, pair][:, i, :],
+                    in_=acc["reset", quarter, pair][:, i, :],
+                    func=ACT.Sigmoid,
+                    bias=bias[:, s : s + 1],
                 )
-                row = half * HALF_ROWS + first
-                nc.sync.dma_start(
-                    out=out_rows[:, row : row + width, s * P : (s + 1) * P], in_=result[:, first : first + width, :]
+
+        def multiply(quarter, pair):
+            gated[quarter, pair] = work.tile([P, 2, QUARTER_COLS], F32, name="gated")
+            nc.vector.tensor_tensor(
+                out=gated[quarter, pair][:], in0=acc["state", quarter, pair], in1=gate[quarter, pair][:], op=ALU.mult
+            )
+
+        def add(quarter, pair, columns):
+            for i in range(2):
+                s = 2 * pair + i
+                nc.vector.scalar_tensor_tensor(
+                    out=before_tanh[quarter, pair][:, i, columns],
+                    in0=acc["cand", quarter, pair][:, i, columns],
+                    scalar=bias[:, SLICES + s : SLICES + s + 1],
+                    in1=gated[quarter, pair][:, i, columns],
+                    op0=ALU.add,
+                    op1=ALU.add,
                 )
+
+        def gates(quarter):
+            for pair in range(SLICES // 2):
+                sigmoid(quarter, pair)
+
+        def combine(quarter, steps):
+            for pair in range(SLICES // 2):
+                multiply(quarter, pair)
+            for pair in range(SLICES // 2):
+                before_tanh[quarter, pair] = work.tile([P, 2, QUARTER_COLS], F32, name="before_tanh")
+            width = QUARTER_COLS // steps
+            for first in range(0, QUARTER_COLS, width):
+                for pair in range(SLICES // 2):
+                    add(quarter, pair, slice(first, first + width))
+
+        def back(quarter):
+            for j in range(QUARTER_ROWS):
+                bank = new_bank()
+                for s in range(SLICES):
+                    nc.tensor.transpose(
+                        bank[:, s * P : (s + 1) * P],
+                        before_tanh[quarter, s // 2][:, s % 2, j * P : (j + 1) * P],
+                        ident[:],
+                    )
+                result = work.tile([P, UNITS], F32, name="result")
+                nc.scalar.activation(out=result[:], in_=bank[:], func=ACT.Tanh)
+                nc.sync.dma_start(out=out_rows[:, quarter * QUARTER_ROWS + j, :], in_=result[:])
 
         x0, h0, x1, h1 = units
         V, S = nc.vector.tensor_copy, nc.scalar.copy
-        low, high = [0, 1], [2, 3]
         keep_warm(WARM_UP)
         turn(x0)
         keep_warm(WARM_BETWEEN)
@@ -275,42 +280,20 @@ def tile_augru_pa_kernel(
         empty(h1, 0, S)
         empty(h1, 2, V)
         quantise(x1)
-        def gates(half, slices):
-            for s in slices:
-                sigmoid(half, s)
-
-        def products(half, slices):
-            for s in slices:
-                multiply(half, s)
-
-        def sums(half, slices):
-            for s in slices:
-                add(half, s)
-
-        passes(0, low)
-        gates(0, low)
-        products(0, low)
-        sums(0, low)
+        passes(0)
+        gates(0)
+        combine(0, 1)
         quantise(h1)
-        passes(0, high)
-        gates(0, high)
-        products(0, high)
-        sums(0, high)
-        back(0, 0, 1)
-        back(0, 1, 1)
-        passes(1, low)
-        gates(1, low)
-        products(1, low)
-        sums(1, low)
-        reset_passes(1, high)
-        gates(1, high)
-        state_passes(1, high)
-        products(1, high)
-        back(0, 2, 1)
-        back(0, 3, 1)
-        back(1, 0, 1)
-        candidate_passes(1, high)
-        sums(1, high)
-        back(1, 1, 1)
-        back(1, 2, 2)
-        back(1, 3, 2)
+        passes(1)
+        gates(1)
+        combine(1, 1)
+        back(0)
+        passes(2)
+        gates(2)
+        combine(2, 1)
+        back(1)
+        passes(3)
+        gates(3)
+        combine(3, 2)
+        back(2)
+        back(3)

from contextlib import ExitStack

import concourse.mybir as mybir
from concourse.masks import make_identity

F32 = mybir.dt.float32
BF16 = mybir.dt.bfloat16
I32 = mybir.dt.int32
U32 = mybir.dt.uint32
U8 = mybir.dt.uint8
FP8X4 = mybir.dt.float8_e4m3fn_x4
ACT = mybir.ActivationFunctionType
ALU = mybir.AluOpType

P = 128
PACK = 4
BATCH = 1024
FEATURES = P * PACK
UNITS = 512
ROWS = BATCH // P
HALVES = 2
HALF_ROWS = ROWS // HALVES
COLS = HALF_ROWS * P
QUARTER_ROWS = 2
QUARTER_COLS = QUARTER_ROWS * P
SLICES = UNITS // P
WARM_UP = 4
WARM_BETWEEN = 2

FLOPS = 2 * 4 * BATCH * FEATURES * UNITS


def tile_augru_pa_kernel(
    tc,
    input_x,
    input_h,
    Wx_r_words,
    Wx_r_scales,
    b_r,
    Wh_r_words,
    Wh_r_scales,
    Wx_h_words,
    Wx_h_scales,
    b_h,
    Wh_h_words,
    Wh_h_scales,
    out,
):
    nc = tc.nc
    weights = {
        "xr": (Wx_r_words, Wx_r_scales),
        "hr": (Wh_r_words, Wh_r_scales),
        "hh": (Wh_h_words, Wh_h_scales),
        "xh": (Wx_h_words, Wx_h_scales),
    }
    activations = {"x": input_x, "h": input_h}
    out_rows = out.rearrange("(p j) n -> p j n", j=ROWS)

    with ExitStack() as ctx:
        ctx.enter_context(tc.manual_schedule())
        keep = ctx.enter_context(tc.tile_pool(name="keep", bufs=1))
        work = ctx.enter_context(tc.tile_pool(name="work", bufs=8))
        banks = ctx.enter_context(tc.psum_pool(name="banks", bufs=8))

        def new_bank():
            bank = banks.tile([P, COLS], F32, name="bank")
            return bank

        raw, sorted_words, grouped, codes, scales = {}, {}, {}, {}, {}
        units = [(name, half) for half in range(HALVES) for name in ("x", "h")]
        for key in units:
            raw[key] = keep.tile([P, HALF_ROWS, FEATURES], BF16, name="raw_%s%d" % key)
            sorted_words[key] = keep.tile([P, HALF_ROWS, 2, P], F32, name="sorted_%s%d" % key)
            grouped[key] = keep.tile([P, COLS * PACK], BF16, name="grouped_%s%d" % key, align_bytes=64)
            codes[key] = keep.tile([P, COLS], U32, name="codes_%s%d" % key, align_bytes=64)
            scales[key] = keep.tile([P, COLS], U8, name="scales_%s%d" % key, align_bytes=64)
        w_codes, w_scales = {}, {}
        for name in weights:
            w_codes[name] = keep.tile([P, UNITS], U32, name="w_codes_" + name, align_bytes=64)
            w_scales[name] = keep.tile([P, UNITS], U8, name="w_scales_" + name, align_bytes=64)
        ident = keep.tile([P, P], F32, name="ident")
        bias_rows = keep.tile([P, P], BF16, name="bias_rows")
        pick = keep.tile([P, 2 * SLICES], BF16, name="pick")
        bias = keep.tile([P, 2 * SLICES], F32, name="bias")
        zeros = keep.tile([P, COLS], BF16, name="zeros")
        warm = keep.tile([P, 2], F32, name="warm")

        make_identity(nc, ident[:])
        nc.vector.memset(bias_rows[:], 0.0)
        nc.scalar.dma_start(out=bias_rows[0:SLICES, :], in_=b_r.rearrange("(s u) -> s u", u=P))
        nc.scalar.dma_start(out=bias_rows[SLICES : 2 * SLICES, :], in_=b_h.rearrange("(s u) -> s u", u=P))
        for name in ("xr", "hh"):
            nc.vector.memset(w_scales[name][:].bitcast(I32), 0)
        nc.vector.memset(zeros[:], 0.0)
        nc.vector.memset(warm[:], 0.0)
        for name in ("hr", "xh"):
            nc.vector.memset(w_scales[name][:].bitcast(I32), 0)
        nc.scalar.activation(out=warm[:, 1:2], in_=warm[:, 0:1], func=ACT.Sigmoid)
        nc.vector.tensor_copy(out=pick[:], in_=ident[:, 0 : 2 * SLICES])

        def load_rows(name, half):
            rows = activations[name].rearrange("(p j) k -> p j k", j=ROWS)
            nc.sync.dma_start(out=raw[name, half][:], in_=rows[:, half * HALF_ROWS : (half + 1) * HALF_ROWS, :])

        def load_codes(name):
            nc.sync.dma_start(
                out=w_codes[name][:].bitcast(I32),
                in_=weights[name][0].rearrange("g p n t -> (g p) (n t)").bitcast(I32),
            )

        def load_scales(name, queue, word, rows=(0, 1, 2, 3)):
            by_r = weights[name][1].rearrange("g (q r) n -> (g r) q n", r=4)
            for r in rows:
                queue.dma_start(out=w_scales[name][r:P:32, :].bitcast(word), in_=by_r[r].bitcast(word))

        load_rows("x", 0)
        load_rows("h", 0)
        load_scales("xr", nc.sync, I32, (0, 1))
        load_rows("x", 1)
        load_rows("h", 1)
        load_scales("hr", nc.sync, I32, (0, 1))
        load_codes("xr")
        load_codes("hr")
        load_scales("hr", nc.sync, I32, (2, 3))
        load_codes("hh")
        load_codes("xh")
        load_scales("hh", nc.sync, I32, (2, 3))
        load_scales("xh", nc.sync, I32)
        load_scales("xr", nc.gpsimd, F32, (2, 3))
        load_scales("hh", nc.gpsimd, F32, (0, 1))

        def keep_warm(count):
            bank = new_bank()
            for repeat in range(count):
                nc.tensor.matmul(out=bank[:], lhsT=zeros[:, 0:P], rhs=zeros[:], start=True, stop=True)

        sorted_keys = []

        def sort_words(key):
            sorted_keys.append(key)
            nc.vector.tensor_copy(
                out=sorted_words[key][:], in_=raw[key][:].bitcast(F32).rearrange("p j (w u) -> p j u w", u=2)
            )

        turned = {}

        def turn(key):
            for first in range(0, HALF_ROWS, 2):
                bank = new_bank()
                by_set = bank[:].rearrange("p (j u b) -> p j u b", j=2, u=2)
                for j in range(2):
                    for u in range(2):
                        if key in sorted_keys:
                            words = sorted_words[key][:, first + j, u, :]
                        else:
                            words = raw[key][:, first + j, :].bitcast(F32)[:, u : FEATURES // 2 : 2]
                        nc.tensor.transpose(by_set[:, j, u, :], words, ident[:])
                turned[key, first] = bank

        def empty(key, first, copy_out):
            pairs_out = grouped[key][:].bitcast(F32).rearrange("p (j b u) -> p j b u", j=HALF_ROWS, u=2)
            copy_out(
                out=pairs_out[:, first : first + 2],
                in_=turned[key, first][:].rearrange("p (j u b) -> p j b u", j=2, u=2),
            )

        def quantise(key):
            nc.vector.quantize_mx(out=codes[key][:].bitcast(FP8X4), scales=scales[key][:], in_=grouped[key][:])

        def bias_columns():
            bank = new_bank()
            nc.tensor.matmul(out=bank[:, 0 : 2 * SLICES], lhsT=bias_rows[:], rhs=pick[:], start=True, stop=True)
            nc.scalar.copy(out=bias[:], in_=bank[:, 0 : 2 * SLICES])

        acc, gate, gated, before_tanh = {}, {}, {}, {}
        sum_of = {"xr": "reset", "hr": "reset", "hh": "state", "xh": "cand"}

        def mx_pass(w_name, quarter, s, start, stop):
            a_name = w_name[0]
            half, columns = quarter // 2, slice(quarter % 2 * QUARTER_COLS, (quarter % 2 + 1) * QUARTER_COLS)
            nc.tensor.matmul_mx(
                out=acc[sum_of[w_name], quarter, s // 2][:, s % 2, :],
                lhsT=w_codes[w_name][:, s * P : (s + 1) * P].bitcast(FP8X4),
                lhsT_scale=w_scales[w_name][:, s * P : (s + 1) * P],
                rhs=codes[a_name, half][:, columns].bitcast(FP8X4),
                rhs_scale=scales[a_name, half][:, columns],
                start=start,
                stop=stop,
            )

        def passes(quarter):
            for kind in ("reset", "state", "cand"):
                for pair in range(SLICES // 2):
                    acc[kind, quarter, pair] = new_bank()[:].rearrange("p (i b) -> p i b", i=2)
            for s in range(SLICES):
                mx_pass("xr", quarter, s, True, False)
                mx_pass("hr", quarter, s, False, True)
            for s in range(SLICES):
                mx_pass("hh", quarter, s, True, True)
            for s in range(SLICES):
                mx_pass("xh", quarter, s, True, True)

        def sigmoid(quarter, pair):
            gate[quarter, pair] = work.tile([P, 2, QUARTER_COLS], F32, name="gate")
            for i in range(2):
                s = 2 * pair + i
                nc.scalar.activation(
                    out=gate[quarter, pair][:, i, :],
                    in_=acc["reset", quarter, pair][:, i, :],
                    func=ACT.Sigmoid,
                    bias=bias[:, s : s + 1],
                )

        def multiply(quarter, pair):
            gated[quarter, pair] = work.tile([P, 2, QUARTER_COLS], F32, name="gated")
            nc.vector.tensor_tensor(
                out=gated[quarter, pair][:], in0=acc["state", quarter, pair], in1=gate[quarter, pair][:], op=ALU.mult
            )

        def add(quarter, pair, columns):
            for i in range(2):
                s = 2 * pair + i
                nc.vector.scalar_tensor_tensor(
                    out=before_tanh[quarter, pair][:, i, columns],
                    in0=acc["cand", quarter, pair][:, i, columns],
                    scalar=bias[:, SLICES + s : SLICES + s + 1],
                    in1=gated[quarter, pair][:, i, columns],
                    op0=ALU.add,
                    op1=ALU.add,
                )

        def gates(quarter):
            for pair in range(SLICES // 2):
                sigmoid(quarter, pair)

        def combine(quarter, steps):
            for pair in range(SLICES // 2):
                multiply(quarter, pair)
            for pair in range(SLICES // 2):
                before_tanh[quarter, pair] = work.tile([P, 2, QUARTER_COLS], F32, name="before_tanh")
            width = QUARTER_COLS // steps
            for first in range(0, QUARTER_COLS, width):
                for pair in range(SLICES // 2):
                    add(quarter, pair, slice(first, first + width))

        def back(quarter):
            for j in range(QUARTER_ROWS):
                bank = new_bank()
                for s in range(SLICES):
                    nc.tensor.transpose(
                        bank[:, s * P : (s + 1) * P],
                        before_tanh[quarter, s // 2][:, s % 2, j * P : (j + 1) * P],
                        ident[:],
                    )
                result = work.tile([P, UNITS], F32, name="result")
                nc.scalar.activation(out=result[:], in_=bank[:], func=ACT.Tanh)
                nc.sync.dma_start(out=out_rows[:, quarter * QUARTER_ROWS + j, :], in_=result[:])

        x0, h0, x1, h1 = units
        V, S = nc.vector.tensor_copy, nc.scalar.copy
        keep_warm(WARM_UP)
        turn(x0)
        keep_warm(WARM_BETWEEN)
        empty(x0, 0, V)
        empty(x0, 2, S)
        bias_columns()
        turn(h0)
        keep_warm(WARM_BETWEEN)
        empty(h0, 0, S)
        empty(h0, 2, S)
        sort_words(x1)
        quantise(x0)
        turn(x1)
        keep_warm(1)
        empty(x1, 0, S)
        sort_words(h1)
        quantise(h0)
        empty(x1, 2, V)
        turn(h1)
        empty(h1, 0, S)
        empty(h1, 2, V)
        quantise(x1)
        passes(0)
        gates(0)
        combine(0, 1)
        quantise(h1)
        passes(1)
        gates(1)
        combine(1, 1)
        back(0)
        passes(2)
        gates(2)
        combine(2, 1)
        back(1)
        passes(3)
        gates(3)
        combine(3, 2)
        back(2)
        back(3)
